import numpy as np
import ml_dtypes

BF16 = ml_dtypes.bfloat16


def bf(x):
    return np.asarray(x, np.float32).astype(BF16)


def f32(x):
    return np.asarray(x, np.float32)


def f64(x):
    return np.asarray(x).astype(np.float64)


def striped(idx):
    return np.tile(idx.reshape(-1, 16).T, (8, 1))


S, D, D2, N, H, K = 256, 128, 256, 512, 128, 4
EPS = 1e-5


def setup_inputs():
    return {"table": bf(np.random.standard_normal((S, D))), "w_left": bf(np.random.standard_normal((D, D)) / np.sqrt(D2)), "w_right": bf(np.random.standard_normal((D, D)) / np.sqrt(D2)), "w_comb": bf(np.random.standard_normal((D2, D)) / np.sqrt(D2)), "b_comb": f32(0.3 * np.random.standard_normal((D, 1))), "w_ff": bf(np.random.standard_normal((D, D)) * np.sqrt(2.0 / D)), "norm_w": f32(1.0 + 0.1 * np.random.standard_normal((D, 1))), "norm_b": f32(0.1 * np.random.standard_normal((D, 1))), "offs": striped(np.concatenate([np.random.permutation(S)[:H] for _ in range(K)]))}


def reference(table, w_left, w_right, w_comb, b_comb, w_ff, norm_w, norm_b, offs):
    idx = offs[:16].T.reshape(-1)
    t = f64(table).T
    info = f64(w_left).T @ t[:, idx[:S]] + f64(w_right).T @ t[:, idx[S:]]
    hid = np.maximum(f64(w_comb)[:D].T @ t + f64(w_comb)[D:].T @ info + f64(b_comb), 0.0)
    added = t + f64(w_ff).T @ hid
    mean = added.mean(axis=1, keepdims=True)
    var = np.square(added - mean).mean(axis=1, keepdims=True)
    return (added - mean) / np.sqrt(var + EPS) * f64(norm_w) + f64(norm_b)

@@ -1,0 +1,130 @@
+import concourse.mybir as mybir
+from concourse.masks import make_identity
+
+P = 128
+S = 256
+N = 512
+C = P
+PIECES = S // C
+PER_COLUMN = 16
+BN_STATS = 6
+EPS = 1e-5
+WARM_MATMULS = 12
+
+BF16, F32, U16 = mybir.dt.bfloat16, mybir.dt.float32, mybir.dt.uint16
+ACT = mybir.ActivationFunctionType
+ALU = mybir.AluOpType
+
+FLOPS = 2 * P * P * (N + 2 * S + S)
+
+
+def tile_messagepassinglayer_kernel(
+    tc, table, w_left, w_right, w_comb, b_comb, w_ff, norm_w, norm_b, offs, out
+):
+    nc = tc.nc
+    with (
+        tc.tile_pool(name="held", bufs=1) as held,
+        tc.psum_pool(name="psum", bufs=1) as psum,
+    ):
+        rows = held.tile([P, PIECES, P], BF16, name="rows")
+        nc.sync.dma_start(rows[:, 0, :], table[0:P, :])
+        nc.scalar.dma_start(rows[:, 1, :], table[P:S, :])
+        offsets = held.tile([P, N // PER_COLUMN], U16, name="offsets")
+        nc.sync.dma_start(offsets[:], offs)
+        left = held.tile([P, P], BF16, name="left")
+        nc.sync.dma_start(left[:], w_left)
+        right = held.tile([P, P], BF16, name="right")
+        nc.sync.dma_start(right[:], w_right)
+        comb = held.tile([P, 2, P], BF16, name="comb")
+        nc.sync.dma_start(comb[:], w_comb.rearrange("(h k) m -> k h m", k=P))
+        feed = held.tile([P, P], BF16, name="feed")
+        nc.sync.dma_start(feed[:], w_ff)
+        bias = held.tile([P, 1], F32, name="bias")
+        gain = held.tile([P, 1], F32, name="gain")
+        shift = held.tile([P, 1], F32, name="shift")
+        with nc.allow_non_contiguous_dma(reason="one float32 to a partition"):
+            nc.sync.dma_start(bias[:], b_comb)
+            nc.sync.dma_start(gain[:], norm_w)
+            nc.sync.dma_start(shift[:], norm_b)
+
+        zeros = held.tile([P, C], BF16, name="zeros")
+        nc.gpsimd.memset(zeros[:], 0.0)
+        idle_work = psum.tile([P, C], F32, name="idle_work")
+        for step in range(WARM_MATMULS):
+            nc.tensor.matmul(idle_work[:], zeros[:], zeros[:], start=True, stop=True)
+
+        identity = held.tile([P, P], BF16, name="identity")
+        make_identity(nc, identity[:])
+        eps = held.tile([P, 1], F32, name="eps")
+        nc.vector.memset(eps[:], EPS)
+        warm = held.tile([P, 1], F32, name="warm")
+        nc.scalar.activation(warm[:], eps[:], ACT.Sqrt)
+
+        flipped = psum.tile([P, S], BF16, name="flipped")
+        for h in range(PIECES):
+            nc.tensor.transpose(flipped[:, h * C : (h + 1) * C], rows[:, h, :], identity[:])
+        window = held.tile([P, S], BF16, name="window")
+        nc.vector.tensor_copy(window[:], flipped[:])
+
+        info_sum = [psum.tile([P, C], F32, name=f"info_sum{h}") for h in range(PIECES)]
+        hid_sum = [psum.tile([P, C], F32, name=f"hid_sum{h}") for h in range(PIECES)]
+        added = [psum.tile([P, C], F32, name=f"added{h}") for h in range(PIECES)]
+        info = [held.tile([P, C], BF16, name=f"info{h}") for h in range(PIECES)]
+        hid = [held.tile([P, C], BF16, name=f"hid{h}") for h in range(PIECES)]
+
+        for h in range(PIECES):
+            nc.tensor.matmul(added[h][:], rows[:, h, :], identity[:], start=True, stop=False)
+
+        k = C // PER_COLUMN
+        for h in range(PIECES):
+            at_left = h * k
+            at_right = S // PER_COLUMN + h * k
+            nc.tensor.matmul(
+                info_sum[h][:],
+                left[:],
+                window[:].indirect(offsets[:, at_left : at_left + k]),
+                start=True,
+                stop=False,
+            )
+            nc.tensor.matmul(
+                info_sum[h][:],
+                right[:],
+                window[:].indirect(offsets[:, at_right : at_right + k]),
+                start=False,
+                stop=True,
+            )
+        nc.scalar.copy(info[0][:], info_sum[0][:])
+        nc.vector.tensor_copy(info[1][:], info_sum[1][:])
+
+        for h in range(PIECES):
+            own = window[:, h * C : (h + 1) * C]
+            nc.tensor.matmul(hid_sum[h][:], comb[:, 0, :], own, start=True, stop=False)
+        for h in range(PIECES):
+            nc.tensor.matmul(hid_sum[h][:], comb[:, 1, :], info[h][:], start=False, stop=True)
+        nc.scalar.activation(hid[0][:], hid_sum[0][:], ACT.Relu, bias=bias[:])
+        nc.vector.tensor_scalar(hid[1][:], hid_sum[1][:], bias[:], 0.0, ALU.add, ALU.max)
+
+        stats = held.tile([P, PIECES, BN_STATS], F32, name="stats")
+        for h in range(PIECES):
+            nc.tensor.matmul(added[h][:], feed[:], hid[h][:], start=False, stop=True)
+            nc.vector.bn_stats(stats[:, h, :], added[h][:])
+
+        mean_var = held.tile([P, 2], F32, name="mean_var")
+        nc.vector.bn_aggr(mean_var[:], stats[:].rearrange("p h s -> p (h s)"))
+        std = held.tile([P, 1], F32, name="std")
+        nc.scalar.activation(std[:], mean_var[:, 1:2], ACT.Sqrt, bias=eps[:])
+        centred = held.tile([P, S], F32, name="centred")
+        for h in range(PIECES):
+            nc.vector.tensor_scalar(
+                centred[:, h * C : (h + 1) * C],
+                added[h][:],
+                mean_var[:, 0:1],
+                gain[:],
+                ALU.subtract,
+                ALU.mult,
+            )
+        rstd = held.tile([P, 1], F32, name="rstd")
+        nc.vector.reciprocal(rstd[:], std[:])
+        result = held.tile([P, S], F32, name="result")
+        nc.vector.tensor_scalar(result[:], centred[:], rstd[:], shift[:], ALU.mult, ALU.add)
+        nc.sync.dma_start(out, result[:])

@@ -9,7 +9,7 @@ PIECES = S // C
 PER_COLUMN = 16
 BN_STATS = 6
 EPS = 1e-5
-WARM_MATMULS = 12
+WARM_MATMULS = 8
 
 BF16, F32, U16 = mybir.dt.bfloat16, mybir.dt.float32, mybir.dt.uint16
 ACT = mybir.ActivationFunctionType

@@ -7,6 +7,7 @@ N = 512
 C = P
 PIECES = S // C
 PER_COLUMN = 16
+LINE = 256
 BN_STATS = 6
 EPS = 1e-5
 WARM_MATMULS = 8
@@ -26,22 +27,22 @@ def tile_messagepassinglayer_kernel(
         tc.tile_pool(name="held", bufs=1) as held,
         tc.psum_pool(name="psum", bufs=1) as psum,
     ):
-        rows = held.tile([P, PIECES, P], BF16, name="rows")
+        rows = held.tile([P, PIECES, P], BF16, name="rows", align_bytes=LINE)
         nc.sync.dma_start(rows[:, 0, :], table[0:P, :])
         nc.scalar.dma_start(rows[:, 1, :], table[P:S, :])
-        offsets = held.tile([P, N // PER_COLUMN], U16, name="offsets")
+        offsets = held.tile([P, N // PER_COLUMN], U16, name="offsets", align_bytes=LINE)
         nc.sync.dma_start(offsets[:], offs)
-        left = held.tile([P, P], BF16, name="left")
+        left = held.tile([P, P], BF16, name="left", align_bytes=LINE)
         nc.sync.dma_start(left[:], w_left)
-        right = held.tile([P, P], BF16, name="right")
+        right = held.tile([P, P], BF16, name="right", align_bytes=LINE)
         nc.sync.dma_start(right[:], w_right)
-        comb = held.tile([P, 2, P], BF16, name="comb")
+        comb = held.tile([P, 2, P], BF16, name="comb", align_bytes=LINE)
         nc.sync.dma_start(comb[:], w_comb.rearrange("(h k) m -> k h m", k=P))
-        feed = held.tile([P, P], BF16, name="feed")
+        feed = held.tile([P, P], BF16, name="feed", align_bytes=LINE)
         nc.sync.dma_start(feed[:], w_ff)
-        bias = held.tile([P, 1], F32, name="bias")
-        gain = held.tile([P, 1], F32, name="gain")
-        shift = held.tile([P, 1], F32, name="shift")
+        bias = held.tile([P, 1], F32, name="bias", align_bytes=LINE)
+        gain = held.tile([P, 1], F32, name="gain", align_bytes=LINE)
+        shift = held.tile([P, 1], F32, name="shift", align_bytes=LINE)
         with nc.allow_non_contiguous_dma(reason="one float32 to a partition"):
             nc.sync.dma_start(bias[:], b_comb)
             nc.sync.dma_start(gain[:], norm_w)
@@ -125,6 +126,6 @@ def tile_messagepassinglayer_kernel(
             )
         rstd = held.tile([P, 1], F32, name="rstd")
         nc.vector.reciprocal(rstd[:], std[:])
-        result = held.tile([P, S], F32, name="result")
+        result = held.tile([P, S], F32, name="result", align_bytes=LINE)
         nc.vector.tensor_scalar(result[:], centred[:], rstd[:], shift[:], ALU.mult, ALU.add)
         nc.sync.dma_start(out, result[:])

import concourse.mybir as mybir
from concourse.masks import make_identity

P = 128
S = 256
N = 512
C = P
PIECES = S // C
PER_COLUMN = 16
LINE = 256
BN_STATS = 6
EPS = 1e-5
WARM_MATMULS = 8

BF16, F32, U16 = mybir.dt.bfloat16, mybir.dt.float32, mybir.dt.uint16
ACT = mybir.ActivationFunctionType
ALU = mybir.AluOpType

FLOPS = 2 * P * P * (N + 2 * S + S)


def tile_messagepassinglayer_kernel(
    tc, table, w_left, w_right, w_comb, b_comb, w_ff, norm_w, norm_b, offs, out
):
    nc = tc.nc
    with (
        tc.tile_pool(name="held", bufs=1) as held,
        tc.psum_pool(name="psum", bufs=1) as psum,
    ):
        rows = held.tile([P, PIECES, P], BF16, name="rows", align_bytes=LINE)
        nc.sync.dma_start(rows[:, 0, :], table[0:P, :])
        nc.scalar.dma_start(rows[:, 1, :], table[P:S, :])
        offsets = held.tile([P, N // PER_COLUMN], U16, name="offsets", align_bytes=LINE)
        nc.sync.dma_start(offsets[:], offs)
        left = held.tile([P, P], BF16, name="left", align_bytes=LINE)
        nc.sync.dma_start(left[:], w_left)
        right = held.tile([P, P], BF16, name="right", align_bytes=LINE)
        nc.sync.dma_start(right[:], w_right)
        comb = held.tile([P, 2, P], BF16, name="comb", align_bytes=LINE)
        nc.sync.dma_start(comb[:], w_comb.rearrange("(h k) m -> k h m", k=P))
        feed = held.tile([P, P], BF16, name="feed", align_bytes=LINE)
        nc.sync.dma_start(feed[:], w_ff)
        bias = held.tile([P, 1], F32, name="bias", align_bytes=LINE)
        gain = held.tile([P, 1], F32, name="gain", align_bytes=LINE)
        shift = held.tile([P, 1], F32, name="shift", align_bytes=LINE)
        with nc.allow_non_contiguous_dma(reason="one float32 to a partition"):
            nc.sync.dma_start(bias[:], b_comb)
            nc.sync.dma_start(gain[:], norm_w)
            nc.sync.dma_start(shift[:], norm_b)

        zeros = held.tile([P, C], BF16, name="zeros")
        nc.gpsimd.memset(zeros[:], 0.0)
        idle_work = psum.tile([P, C], F32, name="idle_work")
        for step in range(WARM_MATMULS):
            nc.tensor.matmul(idle_work[:], zeros[:], zeros[:], start=True, stop=True)

        identity = held.tile([P, P], BF16, name="identity")
        make_identity(nc, identity[:])
        eps = held.tile([P, 1], F32, name="eps")
        nc.vector.memset(eps[:], EPS)
        warm = held.tile([P, 1], F32, name="warm")
        nc.scalar.activation(warm[:], eps[:], ACT.Sqrt)

        flipped = psum.tile([P, S], BF16, name="flipped")
        for h in range(PIECES):
            nc.tensor.transpose(flipped[:, h * C : (h + 1) * C], rows[:, h, :], identity[:])
        window = held.tile([P, S], BF16, name="window")
        nc.vector.tensor_copy(window[:], flipped[:])

        info_sum = [psum.tile([P, C], F32, name=f"info_sum{h}") for h in range(PIECES)]
        hid_sum = [psum.tile([P, C], F32, name=f"hid_sum{h}") for h in range(PIECES)]
        added = [psum.tile([P, C], F32, name=f"added{h}") for h in range(PIECES)]
        info = [held.tile([P, C], BF16, name=f"info{h}") for h in range(PIECES)]
        hid = [held.tile([P, C], BF16, name=f"hid{h}") for h in range(PIECES)]

        for h in range(PIECES):
            nc.tensor.matmul(added[h][:], rows[:, h, :], identity[:], start=True, stop=False)

        k = C // PER_COLUMN
        for h in range(PIECES):
            at_left = h * k
            at_right = S // PER_COLUMN + h * k
            nc.tensor.matmul(
                info_sum[h][:],
                left[:],
                window[:].indirect(offsets[:, at_left : at_left + k]),
                start=True,
                stop=False,
            )
            nc.tensor.matmul(
                info_sum[h][:],
                right[:],
                window[:].indirect(offsets[:, at_right : at_right + k]),
                start=False,
                stop=True,
            )
        nc.scalar.copy(info[0][:], info_sum[0][:])
        nc.vector.tensor_copy(info[1][:], info_sum[1][:])

        for h in range(PIECES):
            own = window[:, h * C : (h + 1) * C]
            nc.tensor.matmul(hid_sum[h][:], comb[:, 0, :], own, start=True, stop=False)
        for h in range(PIECES):
            nc.tensor.matmul(hid_sum[h][:], comb[:, 1, :], info[h][:], start=False, stop=True)
        nc.scalar.activation(hid[0][:], hid_sum[0][:], ACT.Relu, bias=bias[:])
        nc.vector.tensor_scalar(hid[1][:], hid_sum[1][:], bias[:], 0.0, ALU.add, ALU.max)

        stats = held.tile([P, PIECES, BN_STATS], F32, name="stats")
        for h in range(PIECES):
            nc.tensor.matmul(added[h][:], feed[:], hid[h][:], start=False, stop=True)
            nc.vector.bn_stats(stats[:, h, :], added[h][:])

        mean_var = held.tile([P, 2], F32, name="mean_var")
        nc.vector.bn_aggr(mean_var[:], stats[:].rearrange("p h s -> p (h s)"))
        std = held.tile([P, 1], F32, name="std")
        nc.scalar.activation(std[:], mean_var[:, 1:2], ACT.Sqrt, bias=eps[:])
        centred = held.tile([P, S], F32, name="centred")
        for h in range(PIECES):
            nc.vector.tensor_scalar(
                centred[:, h * C : (h + 1) * C],
                added[h][:],
                mean_var[:, 0:1],
                gain[:],
                ALU.subtract,
                ALU.mult,
            )
        rstd = held.tile([P, 1], F32, name="rstd")
        nc.vector.reciprocal(rstd[:], std[:])
        result = held.tile([P, S], F32, name="result", align_bytes=LINE)
        nc.vector.tensor_scalar(result[:], centred[:], rstd[:], shift[:], ALU.mult, ALU.add)
        nc.sync.dma_start(out, result[:])
